import numpy as np
import ml_dtypes


def mxq(x, axis, fmt="e4m3"):
    dtype, down = {"e4m3": (ml_dtypes.float8_e4m3fn, 7), "e5m2": (ml_dtypes.float8_e5m2, 14)}[fmt]
    v = np.moveaxis(np.asarray(x, np.float32).astype(ml_dtypes.bfloat16).astype(np.float64), axis, -1)
    blocks = v.reshape(v.shape[:-1] + (-1, 32))
    amax = np.abs(blocks).max(-1, keepdims=True)
    byte = np.maximum(np.where(amax > 0, np.frexp(amax)[1] - 1 + 127, 0) - down, 1)
    scale = np.exp2(byte - 127.0)
    codes = (blocks / scale).astype(np.float32).astype(dtype).astype(np.float64)
    return np.moveaxis((codes * scale).reshape(v.shape), -1, axis)


WIDE = False


def mx_kscale(k):
    if not WIDE:
        return np.ones(k)
    levels = np.array([10, -10, 5, -5, 0])
    a = np.random.permutation(np.resize(levels, k // 512 * 4)).reshape(k // 512, 4)
    idx = np.arange(k)
    return np.exp2(a[idx // 512, idx % 128 // 32])


BF16 = ml_dtypes.bfloat16


def bf(x):
    return np.asarray(x, np.float32).astype(BF16)


def f64(x):
    return np.asarray(x).astype(np.float64)


B, S, D, H, HS, R = 1, 256, 2048, 16, 128, 32
W = 3 * H * HS
HALF = R // 2
THETA = 10000.0


def rope_tables():
    inv = 1.0 / THETA ** (np.arange(0, R, 2) / R)
    pos = THETA - S + np.arange(S)
    ang = pos[:, None] * inv[None, :]
    return np.cos(ang), np.sin(ang)


def apply_rotary(t, cos, sin):
    re, im = t[..., :HALF], t[..., HALF:]
    c, sn = cos[None, :, None, :], sin[None, :, None, :]
    out = np.stack((re * c - im * sn, re * sn + im * c), axis=-1)
    return out.reshape(t.shape)


def setup_inputs():
    s = mx_kscale(D)
    cos, sin = rope_tables()
    return {"x": bf(np.random.standard_normal((B, S, D)) * s),
            "w_qkv": bf(np.random.standard_normal((D, W)) / np.sqrt(D) / s[:, None]),
            "b_qkv": bf(np.random.standard_normal(W) * 0.3),
            "cos": bf(cos), "sin": bf(sin)}


def reference(x, w_qkv, b_qkv, cos, sin):
    cos, sin = f64(cos), f64(sin)
    qkv = (mxq(f64(x), 2, "e4m3") @ mxq(f64(w_qkv), 0, "e4m3")) + f64(b_qkv)
    qkv = qkv.reshape(B, S, H, 3 * HS)
    q, k, v = qkv[..., :HS], qkv[..., HS:2 * HS], qkv[..., 2 * HS:]
    q_rot = np.concatenate((apply_rotary(q[..., :R], cos, sin), q[..., R:]), axis=3)
    k_rot = np.concatenate((apply_rotary(k[..., :R], cos, sin), k[..., R:]), axis=3)
    return q_rot, k_rot, v

@@ -1,0 +1,230 @@
+from contextlib import ExitStack
+
+import concourse.bass as bass
+import concourse.mybir as mybir
+import concourse.tile as tile
+from concourse.masks import make_identity
+
+FP8X4 = mybir.dt.float8_e4m3fn_x4
+BF16 = mybir.dt.bfloat16
+F32 = mybir.dt.float32
+U32 = mybir.dt.uint32
+U8 = mybir.dt.uint8
+ALU = mybir.AluOpType
+
+P = 128
+TOK = 256
+D = 2048
+HEADS = 16
+HS = 128
+WIDTH = 3 * HEADS * HS
+MT = TOK // P
+PASSES = D // (4 * P)
+HALF = 16
+FLOPS = 2 * TOK * D * WIDTH
+
+PINNED = False
+CHUNKS = [4,4,4,4]
+DEPTH = 5
+X_AFTER = 1
+
+
+def tile_gptneoxattention_pa_kernel(tc, x, w_qkv, b_qkv, cos, sin, out_0, out_1, out_2):
+    nc = tc.nc
+    outs = [out_0, out_1, out_2]
+    with ExitStack() as ctx:
+        consts = ctx.enter_context(tc.tile_pool(name="consts", bufs=1))
+        rawp = ctx.enter_context(tc.tile_pool(name="rawp", bufs=DEPTH))
+        grp_s = ctx.enter_context(tc.tile_pool(name="grp_s", bufs=3))
+        grp_v = ctx.enter_context(tc.tile_pool(name="grp_v", bufs=3))
+        codep = ctx.enter_context(tc.tile_pool(name="codep", bufs=2))
+        stp = ctx.enter_context(tc.tile_pool(name="stp", bufs=2))
+        prodp = ctx.enter_context(tc.tile_pool(name="prodp", bufs=2))
+        psum = ctx.enter_context(tc.psum_pool(name="psum", bufs=8))
+        if PINNED:
+            ctx.enter_context(tc.manual_schedule())
+
+        chunks = []
+        h0 = 0
+        for hc in CHUNKS:
+            chunks.append((h0, hc))
+            h0 += hc
+        pieces = [(c, g) for c in range(len(chunks)) for g in range(PASSES)]
+        n = len(pieces)
+
+        ident = consts.tile([P, P], F32)
+        make_identity(nc, ident[:])
+        cs = consts.tile([P, 2, MT, HALF], BF16)
+        nc.scalar.dma_start(out=cs[:, 0], in_=cos.rearrange("(m p) j -> p m j", p=P))
+        nc.scalar.dma_start(out=cs[:, 1], in_=sin.rearrange("(m p) j -> p m j", p=P))
+        bias_bc = consts.tile([P, WIDTH], BF16)
+        x_codes = consts.tile([P, MT * PASSES * P], U32, align_bytes=64)
+        x_scales = consts.tile([P, MT * PASSES * P], U8, align_bytes=64)
+        ab = consts.tile([P, MT, 2, HALF, 2], F32)
+
+        raws = {}
+        groups = {}
+        codes = {}
+        banks = {}
+
+        def load(i):
+            c, g = pieces[i]
+            h0, hc = chunks[c]
+            raw = rawp.tile([P, 4, 3 * HS * hc], BF16, name="raw")
+            nc.sync.dma_start(
+                out=raw[:],
+                in_=w_qkv[4 * P * g : 4 * P * (g + 1), 3 * HS * h0 : 3 * HS * (h0 + hc)].rearrange(
+                    "(p j) n -> p j n", j=4
+                ),
+            )
+            raws[i] = raw
+            if g == 2:
+                nc.sync.dma_start(
+                    out=bias_bc[:, 3 * HS * h0 : 3 * HS * (h0 + hc)],
+                    in_=b_qkv[3 * HS * h0 : 3 * HS * (h0 + hc)].partition_broadcast(P),
+                )
+
+        def split(i):
+            if i == n - 1:
+                return [("V", (0,)), ("S", (1,)), ("V", (2,))]
+            return [("S", (0, 1)), ("V", (2,))]
+
+        def regroup(i):
+            c, g = pieces[i]
+            h0, hc = chunks[c]
+            src = raws[i][:].rearrange("p t (h y c i) -> p y h c t i", y=3, c=HS // 4, i=4)
+            made = []
+            for eng, types in split(i):
+                pool = grp_s if eng == "S" else grp_v
+                grp = pool.tile([P, len(types), 4 * HS * hc], BF16, name="grp" + eng, align_bytes=64)
+                for k, y in enumerate(types):
+                    dst = grp[:, k, :].rearrange("p (h c i t) -> p h c t i", c=HS // 4, i=4, t=4)
+                    if eng == "S":
+                        nc.scalar.copy(out=dst, in_=src[:, y])
+                    else:
+                        nc.vector.tensor_copy(out=dst, in_=src[:, y])
+                made.append((types, grp))
+            groups[i] = made
+
+        def quantise(i):
+            c, g = pieces[i]
+            h0, hc = chunks[c]
+            if g == 0:
+                wc = codep.tile([P, PASSES, 3, HS * hc], U32, name="wc", align_bytes=64)
+                ws = codep.tile([P, PASSES, 3, HS * hc], U8, name="ws", align_bytes=64)
+                codes[c] = (wc, ws)
+            wc, ws = codes[c]
+            for types, grp in groups[i]:
+                y0, y1 = types[0], types[-1] + 1
+                nc.vector.quantize_mx(
+                    out=wc[:, g, y0:y1, :].rearrange("p y n -> p (y n)").bitcast(FP8X4),
+                    scales=ws[:, g, y0:y1, :].rearrange("p y n -> p (y n)"),
+                    in_=grp[:].rearrange("p y n -> p (y n)"),
+                )
+
+        def matmuls(i):
+            c, g = pieces[i]
+            h0, hc = chunks[c]
+            wc, ws = codes[c]
+            for m in range(MT):
+                for y in range(3):
+                    if g == 0:
+                        banks[(c, m, y)] = psum.tile([P, HS * hc], F32, name="bank")
+                    lo = (m * PASSES + g) * P
+                    nc.tensor.matmul_mx(
+                        out=banks[(c, m, y)][:],
+                        lhsT=x_codes[:, lo : lo + P].bitcast(FP8X4),
+                        lhsT_scale=x_scales[:, lo : lo + P],
+                        rhs=wc[:, g, y, :].bitcast(FP8X4),
+                        rhs_scale=ws[:, g, y, :],
+                        start=(g == 0),
+                        stop=(g == PASSES - 1),
+                    )
+
+        def finish(c):
+            h0, hc = chunks[c]
+            st = stp.tile([P, MT, 3, HS * hc], F32, name="st")
+            bias_v = bias_bc[:, 3 * HS * h0 : 3 * HS * (h0 + hc)].rearrange("p (h y f) -> p y h f", y=3, f=HS)
+            for m in range(MT):
+                for y in range(3):
+                    nc.vector.tensor_tensor(
+                        out=st[:, m, y, :].rearrange("p (h f) -> p h f", f=HS),
+                        in0=banks[(c, m, y)][:].rearrange("p (h f) -> p h f", f=HS),
+                        in1=bias_v[:, y],
+                        op=ALU.add,
+                    )
+                    if y == 1:
+                        rot = st[:, m, 0:2, :].rearrange("p y (h f) -> p (y h) f", f=HS)[:, :, 0 : 2 * HALF]
+                        prod = prodp.tile([P, 2 * hc, 2 * HALF, 2], F32, name="prod")
+                        nc.vector.tensor_tensor(
+                            out=prod[:],
+                            in0=rot.unsqueeze(3).to_broadcast([P, 2 * hc, 2 * HALF, 2]),
+                            in1=ab[:, m].rearrange("p a j e -> p (a j) e").unsqueeze(1).to_broadcast([P, 2 * hc, 2 * HALF, 2]),
+                            op=ALU.mult,
+                        )
+                        flat = prod[:].rearrange("p g a e -> p g (a e)")
+                        nc.vector.tensor_tensor(
+                            out=rot, in0=flat[:, :, 0 : 2 * HALF], in1=flat[:, :, 2 * HALF : 4 * HALF], op=ALU.add
+                        )
+                        for yy in range(2):
+                            nc.sync.dma_start(
+                                out=outs[yy][0, P * m : P * (m + 1), h0 : h0 + hc, :].rearrange("p h f -> p (h f)"),
+                                in_=st[:, m, yy, :],
+                            )
+                nc.sync.dma_start(
+                    out=outs[2][0, P * m : P * (m + 1), h0 : h0 + hc, :].rearrange("p h f -> p (h f)"),
+                    in_=st[:, m, 2, :],
+                )
+
+        x_sb = []
+
+        def load_x():
+            for m in range(MT):
+                xs = consts.tile([P, D], BF16, name="x_sb%d" % m)
+                nc.sync.dma_start(out=xs[:], in_=x[0, P * m : P * (m + 1), :])
+                x_sb.append(xs)
+
+        def prepare_x():
+            nc.vector.tensor_copy(out=ab[:, :, 0, :, 0], in_=cs[:, 0])
+            nc.vector.tensor_copy(out=ab[:, :, 0, :, 1], in_=cs[:, 1])
+            nc.vector.tensor_scalar_mul(out=ab[:, :, 1, :, 0], in0=cs[:, 1], scalar1=-1.0)
+            nc.vector.tensor_copy(out=ab[:, :, 1, :, 1], in_=cs[:, 0])
+            gxs = []
+            for m in range(MT):
+                words = x_sb[m][:].bitcast(F32).rearrange("p (g c u) -> p g u c", g=PASSES, u=2)
+                gx = consts.tile([P, 4 * PASSES * P], BF16, name="gx%d" % m, align_bytes=64)
+                gxw = gx[:].bitcast(F32).rearrange("p (g r u) -> p g r u", g=PASSES, u=2)
+                for gp in range(PASSES // 2):
+                    xt = psum.tile([P, 2, 2, P], F32, name="bank")
+                    for gl in range(2):
+                        for u in range(2):
+                            nc.tensor.transpose(xt[:, gl, u, :], words[:, 2 * gp + gl, u, :], ident[:])
+                    if gp == 0:
+                        nc.vector.tensor_copy(out=gxw[:, 2 * gp : 2 * gp + 2], in_=xt[:].rearrange("p g u r -> p g r u"))
+                    else:
+                        nc.scalar.copy(out=gxw[:, 2 * gp : 2 * gp + 2], in_=xt[:].rearrange("p g u r -> p g r u"))
+                gxs.append(gx)
+            for m in range(MT):
+                lo = m * PASSES * P
+                nc.vector.quantize_mx(
+                    out=x_codes[:, lo : lo + PASSES * P].bitcast(FP8X4),
+                    scales=x_scales[:, lo : lo + PASSES * P],
+                    in_=gxs[m][:],
+                )
+
+        for i in range(DEPTH):
+            if i == X_AFTER:
+                load_x()
+            load(i)
+        for i in range(n + 1):
+            if i == 1:
+                prepare_x()
+            if i >= 1:
+                quantise(i - 1)
+                matmuls(i - 1)
+            if i < n:
+                regroup(i)
+                if i + DEPTH < n:
+                    load(i + DEPTH)
+            if i >= 1 and pieces[i - 1][1] == PASSES - 1:
+                finish(pieces[i - 1][0])

@@ -62,6 +62,26 @@ def tile_gptneoxattention_pa_kernel(tc, x, w_qkv, b_qkv, cos, sin, out_0, out_1,
         x_scales = consts.tile([P, MT * PASSES * P], U8, align_bytes=64)
         ab = consts.tile([P, MT, 2, HALF, 2], F32)
 
+        ones = consts.tile([P, P], BF16)
+        nc.vector.memset(ones[:], 1.0)
+        brow = rawp.tile([P, 4, 3 * HS * 4], BF16, name="raw")
+        brow_flat = brow[:].rearrange("p t n -> p (t n)")
+        nc.vector.memset(brow_flat.bitcast(F32), 0.0)
+        nc.scalar.dma_start(out=brow_flat[0:1, :], in_=b_qkv.rearrange("(o n) -> o n", o=1))
+
+        def spread_bias():
+            for k in range(WIDTH // 1024):
+                pb = psum.tile([P, 1024], BF16, name="bank")
+                for j in range(2):
+                    lo = 1024 * k + 512 * j
+                    nc.tensor.matmul(
+                        out=pb[:, 512 * j : 512 * (j + 1)], lhsT=ones[:], rhs=brow_flat[:, lo : lo + 512], start=True, stop=True
+                    )
+                if k % 2 == 0:
+                    nc.scalar.copy(out=bias_bc[:, 1024 * k : 1024 * (k + 1)], in_=pb[:])
+                else:
+                    nc.vector.tensor_copy(out=bias_bc[:, 1024 * k : 1024 * (k + 1)], in_=pb[:])
+
         raws = {}
         groups = {}
         codes = {}
@@ -78,7 +98,7 @@ def tile_gptneoxattention_pa_kernel(tc, x, w_qkv, b_qkv, cos, sin, out_0, out_1,
                 ),
             )
             raws[i] = raw
-            if g == 2:
+            if g == 99:
                 nc.sync.dma_start(
                     out=bias_bc[:, 3 * HS * h0 : 3 * HS * (h0 + hc)],
                     in_=b_qkv[3 * HS * h0 : 3 * HS * (h0 + hc)].partition_broadcast(P),
@@ -212,10 +232,12 @@ def tile_gptneoxattention_pa_kernel(tc, x, w_qkv, b_qkv, cos, sin, out_0, out_1,
                     in_=gxs[m][:],
                 )
 
-        for i in range(DEPTH):
+        for i in range(DEPTH - 1):
             if i == X_AFTER:
                 load_x()
             load(i)
+        spread_bias()
+        load(DEPTH - 1)
         for i in range(n + 1):
             if i == 1:
                 prepare_x()

@@ -1,8 +1,6 @@
 from contextlib import ExitStack
 
-import concourse.bass as bass
 import concourse.mybir as mybir
-import concourse.tile as tile
 from concourse.masks import make_identity
 
 FP8X4 = mybir.dt.float8_e4m3fn_x4
@@ -24,9 +22,15 @@ HALF = 16
 FLOPS = 2 * TOK * D * WIDTH
 
 PINNED = False
-CHUNKS = [4,4,4,4]
+CHUNKS = [2,4,4,4,2]
+V_TYPES = [1,1,1,1,1,1,1,1,1,1,1,1,1,1,1,1,0,0,0,0]
 DEPTH = 5
-X_AFTER = 1
+LAG = 1
+X_AFTER = 0
+X_STEP = 1
+B_STEP = 1
+B_ENG = "V"
+ORDER = [(0, 0), (0, 1), (1, 0), (1, 1), (0, 2), (1, 2)]
 
 
 def tile_gptneoxattention_pa_kernel(tc, x, w_qkv, b_qkv, cos, sin, out_0, out_1, out_2):
@@ -35,59 +39,51 @@ def tile_gptneoxattention_pa_kernel(tc, x, w_qkv, b_qkv, cos, sin, out_0, out_1,
     with ExitStack() as ctx:
         consts = ctx.enter_context(tc.tile_pool(name="consts", bufs=1))
         rawp = ctx.enter_context(tc.tile_pool(name="rawp", bufs=DEPTH))
-        grp_s = ctx.enter_context(tc.tile_pool(name="grp_s", bufs=3))
-        grp_v = ctx.enter_context(tc.tile_pool(name="grp_v", bufs=3))
+        grpp = ctx.enter_context(tc.tile_pool(name="grpp", bufs=8))
         codep = ctx.enter_context(tc.tile_pool(name="codep", bufs=2))
-        stp = ctx.enter_context(tc.tile_pool(name="stp", bufs=2))
-        prodp = ctx.enter_context(tc.tile_pool(name="prodp", bufs=2))
-        psum = ctx.enter_context(tc.psum_pool(name="psum", bufs=8))
+        stp = ctx.enter_context(tc.tile_pool(name="stp", bufs=1))
+        prodp = ctx.enter_context(tc.tile_pool(name="prodp", bufs=1))
+        psum = ctx.enter_context(tc.psum_pool(name="psum", bufs=1))
         if PINNED:
             ctx.enter_context(tc.manual_schedule())
 
         chunks = []
-        h0 = 0
+        first = 0
         for hc in CHUNKS:
-            chunks.append((h0, hc))
-            h0 += hc
+            chunks.append((first, hc))
+            first += hc
         pieces = [(c, g) for c in range(len(chunks)) for g in range(PASSES)]
         n = len(pieces)
 
-        ident = consts.tile([P, P], F32)
-        make_identity(nc, ident[:])
+        b12 = consts.tile([P, 512], BF16)
+        nc.vector.memset(b12[:].bitcast(F32), 0.0)
+        nc.sync.dma_start(out=b12[0 : WIDTH // 512, :], in_=b_qkv.rearrange("(k n) -> k n", n=512))
         cs = consts.tile([P, 2, MT, HALF], BF16)
         nc.scalar.dma_start(out=cs[:, 0], in_=cos.rearrange("(m p) j -> p m j", p=P))
         nc.scalar.dma_start(out=cs[:, 1], in_=sin.rearrange("(m p) j -> p m j", p=P))
+        identb = consts.tile([P, P], BF16)
+        make_identity(nc, identb[:])
+        ident = consts.tile([P, P], F32)
+        make_identity(nc, ident[:])
         bias_bc = consts.tile([P, WIDTH], BF16)
         x_codes = consts.tile([P, MT * PASSES * P], U32, align_bytes=64)
         x_scales = consts.tile([P, MT * PASSES * P], U8, align_bytes=64)
         ab = consts.tile([P, MT, 2, HALF, 2], F32)
-
-        ones = consts.tile([P, P], BF16)
-        nc.vector.memset(ones[:], 1.0)
-        brow = rawp.tile([P, 4, 3 * HS * 4], BF16, name="raw")
-        brow_flat = brow[:].rearrange("p t n -> p (t n)")
-        nc.vector.memset(brow_flat.bitcast(F32), 0.0)
-        nc.scalar.dma_start(out=brow_flat[0:1, :], in_=b_qkv.rearrange("(o n) -> o n", o=1))
-
-        def spread_bias():
-            for k in range(WIDTH // 1024):
-                pb = psum.tile([P, 1024], BF16, name="bank")
-                for j in range(2):
-                    lo = 1024 * k + 512 * j
-                    nc.tensor.matmul(
-                        out=pb[:, 512 * j : 512 * (j + 1)], lhsT=ones[:], rhs=brow_flat[:, lo : lo + 512], start=True, stop=True
-                    )
-                if k % 2 == 0:
-                    nc.scalar.copy(out=bias_bc[:, 1024 * k : 1024 * (k + 1)], in_=pb[:])
-                else:
-                    nc.vector.tensor_copy(out=bias_bc[:, 1024 * k : 1024 * (k + 1)], in_=pb[:])
+        abrep = {}
+        for hc in sorted(set(CHUNKS)):
+            abrep[hc] = consts.tile([P, MT, hc, 4 * HALF], F32, name="abrep%d" % hc)
 
         raws = {}
         groups = {}
         codes = {}
         banks = {}
+        state = {"next": 0}
 
-        def load(i):
+        def load_next():
+            i = state["next"]
+            if i >= n:
+                return
+            state["next"] = i + 1
             c, g = pieces[i]
             h0, hc = chunks[c]
             raw = rawp.tile([P, 4, 3 * HS * hc], BF16, name="raw")
@@ -98,32 +94,20 @@ def tile_gptneoxattention_pa_kernel(tc, x, w_qkv, b_qkv, cos, sin, out_0, out_1,
                 ),
             )
             raws[i] = raw
-            if g == 99:
-                nc.sync.dma_start(
-                    out=bias_bc[:, 3 * HS * h0 : 3 * HS * (h0 + hc)],
-                    in_=b_qkv[3 * HS * h0 : 3 * HS * (h0 + hc)].partition_broadcast(P),
-                )
-
-        def split(i):
-            if i == n - 1:
-                return [("V", (0,)), ("S", (1,)), ("V", (2,))]
-            return [("S", (0, 1)), ("V", (2,))]
 
         def regroup(i):
             c, g = pieces[i]
             h0, hc = chunks[c]
             src = raws[i][:].rearrange("p t (h y c i) -> p y h c t i", y=3, c=HS // 4, i=4)
             made = []
-            for eng, types in split(i):
-                pool = grp_s if eng == "S" else grp_v
-                grp = pool.tile([P, len(types), 4 * HS * hc], BF16, name="grp" + eng, align_bytes=64)
-                for k, y in enumerate(types):
-                    dst = grp[:, k, :].rearrange("p (h c i t) -> p h c t i", c=HS // 4, i=4, t=4)
-                    if eng == "S":
-                        nc.scalar.copy(out=dst, in_=src[:, y])
-                    else:
-                        nc.vector.tensor_copy(out=dst, in_=src[:, y])
-                made.append((types, grp))
+            for y in range(3):
+                grp = grpp.tile([P, 4 * HS * hc], BF16, name="grp", align_bytes=64)
+                dst = grp[:].rearrange("p (h c i t) -> p h c t i", c=HS // 4, i=4, t=4)
+                if y >= 3 - V_TYPES[i]:
+                    nc.vector.tensor_copy(out=dst, in_=src[:, y])
+                else:
+                    nc.scalar.copy(out=dst, in_=src[:, y])
+                made.append(grp)
             groups[i] = made
 
         def quantise(i):
@@ -134,96 +118,114 @@ def tile_gptneoxattention_pa_kernel(tc, x, w_qkv, b_qkv, cos, sin, out_0, out_1,
                 ws = codep.tile([P, PASSES, 3, HS * hc], U8, name="ws", align_bytes=64)
                 codes[c] = (wc, ws)
             wc, ws = codes[c]
-            for types, grp in groups[i]:
-                y0, y1 = types[0], types[-1] + 1
-                nc.vector.quantize_mx(
-                    out=wc[:, g, y0:y1, :].rearrange("p y n -> p (y n)").bitcast(FP8X4),
-                    scales=ws[:, g, y0:y1, :].rearrange("p y n -> p (y n)"),
-                    in_=grp[:].rearrange("p y n -> p (y n)"),
-                )
+            for y in range(3):
+                nc.vector.quantize_mx(out=wc[:, g, y, :].bitcast(FP8X4), scales=ws[:, g, y, :], in_=groups[i][y][:])
 
         def matmuls(i):
             c, g = pieces[i]
             h0, hc = chunks[c]
             wc, ws = codes[c]
-            for m in range(MT):
-                for y in range(3):
-                    if g == 0:
-                        banks[(c, m, y)] = psum.tile([P, HS * hc], F32, name="bank")
-                    lo = (m * PASSES + g) * P
-                    nc.tensor.matmul_mx(
-                        out=banks[(c, m, y)][:],
-                        lhsT=x_codes[:, lo : lo + P].bitcast(FP8X4),
-                        lhsT_scale=x_scales[:, lo : lo + P],
-                        rhs=wc[:, g, y, :].bitcast(FP8X4),
-                        rhs_scale=ws[:, g, y, :],
-                        start=(g == 0),
-                        stop=(g == PASSES - 1),
-                    )
+            for m, y in ORDER:
+                if g == 0:
+                    banks[(c, m, y)] = psum.tile([P, HS * hc], F32, name="acc%d%d" % (m, y))
+                lo = (m * PASSES + g) * P
+                nc.tensor.matmul_mx(
+                    out=banks[(c, m, y)][:],
+                    lhsT=x_codes[:, lo : lo + P].bitcast(FP8X4),
+                    lhsT_scale=x_scales[:, lo : lo + P],
+                    rhs=wc[:, g, y, :].bitcast(FP8X4),
+                    rhs_scale=ws[:, g, y, :],
+                    start=(g == 0),
+                    stop=(g == PASSES - 1),
+                )
 
         def finish(c):
             h0, hc = chunks[c]
-            st = stp.tile([P, MT, 3, HS * hc], F32, name="st")
+            st = stp.tile([P, 3, MT, HS * hc], F32, name="st%d" % c)
             bias_v = bias_bc[:, 3 * HS * h0 : 3 * HS * (h0 + hc)].rearrange("p (h y f) -> p y h f", y=3, f=HS)
-            for m in range(MT):
-                for y in range(3):
-                    nc.vector.tensor_tensor(
-                        out=st[:, m, y, :].rearrange("p (h f) -> p h f", f=HS),
-                        in0=banks[(c, m, y)][:].rearrange("p (h f) -> p h f", f=HS),
-                        in1=bias_v[:, y],
-                        op=ALU.add,
-                    )
-                    if y == 1:
-                        rot = st[:, m, 0:2, :].rearrange("p y (h f) -> p (y h) f", f=HS)[:, :, 0 : 2 * HALF]
-                        prod = prodp.tile([P, 2 * hc, 2 * HALF, 2], F32, name="prod")
-                        nc.vector.tensor_tensor(
-                            out=prod[:],
-                            in0=rot.unsqueeze(3).to_broadcast([P, 2 * hc, 2 * HALF, 2]),
-                            in1=ab[:, m].rearrange("p a j e -> p (a j) e").unsqueeze(1).to_broadcast([P, 2 * hc, 2 * HALF, 2]),
-                            op=ALU.mult,
-                        )
-                        flat = prod[:].rearrange("p g a e -> p g (a e)")
-                        nc.vector.tensor_tensor(
-                            out=rot, in0=flat[:, :, 0 : 2 * HALF], in1=flat[:, :, 2 * HALF : 4 * HALF], op=ALU.add
-                        )
-                        for yy in range(2):
-                            nc.sync.dma_start(
-                                out=outs[yy][0, P * m : P * (m + 1), h0 : h0 + hc, :].rearrange("p h f -> p (h f)"),
-                                in_=st[:, m, yy, :],
-                            )
-                nc.sync.dma_start(
-                    out=outs[2][0, P * m : P * (m + 1), h0 : h0 + hc, :].rearrange("p h f -> p (h f)"),
-                    in_=st[:, m, 2, :],
+
+            def leave(m, y):
+                nc.vector.tensor_tensor(
+                    out=st[:, y, m, :].rearrange("p (h f) -> p h f", f=HS),
+                    in0=banks[(c, m, y)][:].rearrange("p (h f) -> p h f", f=HS),
+                    in1=bias_v[:, y],
+                    op=ALU.add,
                 )
 
-        x_sb = []
+            def store(y):
+                nc.sync.dma_start(
+                    out=outs[y][0, :, h0 : h0 + hc, :].rearrange("(m p) h f -> p m (h f)", p=P), in_=st[:, y]
+                )
 
-        def load_x():
-            for m in range(MT):
-                xs = consts.tile([P, D], BF16, name="x_sb%d" % m)
-                nc.sync.dma_start(out=xs[:], in_=x[0, P * m : P * (m + 1), :])
-                x_sb.append(xs)
+            for m, y in ORDER[0:4]:
+                leave(m, y)
+            shape = [P, 2, MT * hc, 2 * HALF, 2]
+            prod = prodp.tile(shape, F32, name="prod")
+            nc.vector.tensor_tensor(
+                out=prod[:],
+                in0=st[:, 0:2].rearrange("p y m (h f) -> p y (m h) f", f=HS)[:, :, :, 0 : 2 * HALF].unsqueeze(4).to_broadcast(shape),
+                in1=abrep[hc][:].rearrange("p m h (a e) -> p (m h) a e", e=2).unsqueeze(1).to_broadcast(shape),
+                op=ALU.mult,
+            )
+            leave(0, 2)
+            flat = prod[:].rearrange("p y g a e -> p (y g) (a e)")
+            nc.vector.tensor_tensor(
+                out=st[:, 0:2].rearrange("p y m (h f) -> p (y m h) f", f=HS)[:, :, 0 : 2 * HALF],
+                in0=flat[:, :, 0 : 2 * HALF],
+                in1=flat[:, :, 2 * HALF : 4 * HALF],
+                op=ALU.add,
+            )
+            store(0)
+            store(1)
+            leave(1, 2)
+            store(2)
 
-        def prepare_x():
-            nc.vector.tensor_copy(out=ab[:, :, 0, :, 0], in_=cs[:, 0])
-            nc.vector.tensor_copy(out=ab[:, :, 0, :, 1], in_=cs[:, 1])
-            nc.vector.tensor_scalar_mul(out=ab[:, :, 1, :, 0], in0=cs[:, 1], scalar1=-1.0)
-            nc.vector.tensor_copy(out=ab[:, :, 1, :, 1], in_=cs[:, 0])
-            gxs = []
+        x_sb = None
+        for i in range(DEPTH - 1):
+            load_next()
+            if i == X_AFTER:
+                x_sb = rawp.tile([P, MT, D], BF16, name="raw")
+                for m in range(MT):
+                    nc.sync.dma_start(out=x_sb[:, m, :], in_=x[0, P * m : P * (m + 1), :])
+
+        pbs = []
+        for k in range(WIDTH // 1024):
+            m, y = ORDER[k]
+            pb = psum.tile([P, 1024], BF16, name="pb%d" % k, tag="acc%d%d" % (m, y))
+            for j in range(2):
+                r = 2 * k + j
+                nc.tensor.matmul(
+                    out=pb[:, 512 * j : 512 * (j + 1)],
+                    lhsT=identb[:, r : r + 1].to_broadcast([P, P]),
+                    rhs=b12[:],
+                    start=True,
+                    stop=True,
+                )
+            pbs.append(pb)
+
+        def bias_out():
+            for k in range(WIDTH // 1024):
+                if B_ENG == "S":
+                    nc.scalar.copy(out=bias_bc[:, 1024 * k : 1024 * (k + 1)], in_=pbs[k][:])
+                else:
+                    nc.vector.tensor_copy(out=bias_bc[:, 1024 * k : 1024 * (k + 1)], in_=pbs[k][:])
+
+        gxs = []
+
+        def x_transposes():
             for m in range(MT):
-                words = x_sb[m][:].bitcast(F32).rearrange("p (g c u) -> p g u c", g=PASSES, u=2)
-                gx = consts.tile([P, 4 * PASSES * P], BF16, name="gx%d" % m, align_bytes=64)
+                words = x_sb[:, m, :].bitcast(F32).rearrange("p (g c u) -> p g u c", g=PASSES, u=2)
+                gx = grpp.tile([P, 4 * PASSES * P], BF16, name="grp", align_bytes=64)
                 gxw = gx[:].bitcast(F32).rearrange("p (g r u) -> p g r u", g=PASSES, u=2)
                 for gp in range(PASSES // 2):
-                    xt = psum.tile([P, 2, 2, P], F32, name="bank")
+                    xt = psum.tile([P, 2, 2, P], F32, name="pt", bufs=2)
                     for gl in range(2):
                         for u in range(2):
                             nc.tensor.transpose(xt[:, gl, u, :], words[:, 2 * gp + gl, u, :], ident[:])
-                    if gp == 0:
-                        nc.vector.tensor_copy(out=gxw[:, 2 * gp : 2 * gp + 2], in_=xt[:].rearrange("p g u r -> p g r u"))
-                    else:
-                        nc.scalar.copy(out=gxw[:, 2 * gp : 2 * gp + 2], in_=xt[:].rearrange("p g u r -> p g r u"))
+                    nc.vector.tensor_copy(out=gxw[:, 2 * gp : 2 * gp + 2], in_=xt[:].rearrange("p g u r -> p g r u"))
                 gxs.append(gx)
+
+        def x_quantise():
             for m in range(MT):
                 lo = m * PASSES * P
                 nc.vector.quantize_mx(
@@ -232,21 +234,36 @@ def tile_gptneoxattention_pa_kernel(tc, x, w_qkv, b_qkv, cos, sin, out_0, out_1,
                     in_=gxs[m][:],
                 )
 
-        for i in range(DEPTH - 1):
-            if i == X_AFTER:
-                load_x()
-            load(i)
-        spread_bias()
-        load(DEPTH - 1)
-        for i in range(n + 1):
-            if i == 1:
-                prepare_x()
-            if i >= 1:
-                quantise(i - 1)
-                matmuls(i - 1)
+        def tables():
+            nc.vector.tensor_copy(out=ab[:, :, 0, :, 0], in_=cs[:, 0])
+            nc.vector.tensor_copy(out=ab[:, :, 0, :, 1], in_=cs[:, 1])
+            nc.vector.tensor_scalar_mul(out=ab[:, :, 1, :, 0], in0=cs[:, 1], scalar1=-1.0)
+            nc.vector.tensor_copy(out=ab[:, :, 1, :, 1], in_=cs[:, 0])
+            for hc in sorted(set(CHUNKS)):
+                nc.vector.tensor_copy(
+                    out=abrep[hc][:],
+                    in_=ab[:].rearrange("p m a j e -> p m (a j e)").unsqueeze(2).to_broadcast([P, MT, hc, 4 * HALF]),
+                )
+
+        pend = []
+        for i in range(n + LAG):
             if i < n:
                 regroup(i)
-                if i + DEPTH < n:
-                    load(i + DEPTH)
-            if i >= 1 and pieces[i - 1][1] == PASSES - 1:
-                finish(pieces[i - 1][0])
+                load_next()
+            if i == X_STEP - 1:
+                x_transposes()
+                load_next()
+            if i == B_STEP:
+                bias_out()
+                tables()
+            if i == X_STEP:
+                x_quantise()
+            if i - LAG >= 0:
+                quantise(i - LAG)
+                pend.append(i - LAG)
+            if i >= X_STEP and i >= B_STEP:
+                for j in pend:
+                    matmuls(j)
+                    if pieces[j][1] == PASSES - 1:
+                        finish(pieces[j][0])
+                pend = []

@@ -23,14 +23,9 @@ FLOPS = 2 * TOK * D * WIDTH
 
 PINNED = False
 CHUNKS = [2,4,4,4,2]
-V_TYPES = [1,1,1,1,1,1,1,1,1,1,1,1,1,1,1,1,0,0,0,0]
 DEPTH = 5
-LAG = 1
-X_AFTER = 0
 X_STEP = 1
-B_STEP = 1
-B_ENG = "V"
-ORDER = [(0, 0), (0, 1), (1, 0), (1, 1), (0, 2), (1, 2)]
+B_STEP = 3
 
 
 def tile_gptneoxattention_pa_kernel(tc, x, w_qkv, b_qkv, cos, sin, out_0, out_1, out_2):
@@ -39,7 +34,7 @@ def tile_gptneoxattention_pa_kernel(tc, x, w_qkv, b_qkv, cos, sin, out_0, out_1,
     with ExitStack() as ctx:
         consts = ctx.enter_context(tc.tile_pool(name="consts", bufs=1))
         rawp = ctx.enter_context(tc.tile_pool(name="rawp", bufs=DEPTH))
-        grpp = ctx.enter_context(tc.tile_pool(name="grpp", bufs=8))
+        grpp = ctx.enter_context(tc.tile_pool(name="grpp", bufs=3))
         codep = ctx.enter_context(tc.tile_pool(name="codep", bufs=2))
         stp = ctx.enter_context(tc.tile_pool(name="stp", bufs=1))
         prodp = ctx.enter_context(tc.tile_pool(name="prodp", bufs=1))
@@ -54,24 +49,6 @@ def tile_gptneoxattention_pa_kernel(tc, x, w_qkv, b_qkv, cos, sin, out_0, out_1,
             first += hc
         pieces = [(c, g) for c in range(len(chunks)) for g in range(PASSES)]
         n = len(pieces)
-
-        b12 = consts.tile([P, 512], BF16)
-        nc.vector.memset(b12[:].bitcast(F32), 0.0)
-        nc.sync.dma_start(out=b12[0 : WIDTH // 512, :], in_=b_qkv.rearrange("(k n) -> k n", n=512))
-        cs = consts.tile([P, 2, MT, HALF], BF16)
-        nc.scalar.dma_start(out=cs[:, 0], in_=cos.rearrange("(m p) j -> p m j", p=P))
-        nc.scalar.dma_start(out=cs[:, 1], in_=sin.rearrange("(m p) j -> p m j", p=P))
-        identb = consts.tile([P, P], BF16)
-        make_identity(nc, identb[:])
-        ident = consts.tile([P, P], F32)
-        make_identity(nc, ident[:])
-        bias_bc = consts.tile([P, WIDTH], BF16)
-        x_codes = consts.tile([P, MT * PASSES * P], U32, align_bytes=64)
-        x_scales = consts.tile([P, MT * PASSES * P], U8, align_bytes=64)
-        ab = consts.tile([P, MT, 2, HALF, 2], F32)
-        abrep = {}
-        for hc in sorted(set(CHUNKS)):
-            abrep[hc] = consts.tile([P, MT, hc, 4 * HALF], F32, name="abrep%d" % hc)
 
         raws = {}
         groups = {}
@@ -95,46 +72,77 @@ def tile_gptneoxattention_pa_kernel(tc, x, w_qkv, b_qkv, cos, sin, out_0, out_1,
             )
             raws[i] = raw
 
+        b12 = consts.tile([P, 512], BF16)
+        nc.vector.memset(b12[:].bitcast(F32), 0.0)
+        load_next()
+        nc.sync.dma_start(out=b12[0 : WIDTH // 512, :], in_=b_qkv.rearrange("(k n) -> k n", n=512))
+        x_sb = rawp.tile([P, MT, D], BF16, name="raw")
+        for m in range(MT):
+            nc.sync.dma_start(out=x_sb[:, m, :], in_=x[0, P * m : P * (m + 1), :])
+        for i in range(DEPTH - 2):
+            load_next()
+        cs = consts.tile([P, 2, MT, HALF], BF16)
+        nc.scalar.dma_start(out=cs[:, 0], in_=cos.rearrange("(m p) j -> p m j", p=P))
+        nc.scalar.dma_start(out=cs[:, 1], in_=sin.rearrange("(m p) j -> p m j", p=P))
+        ident = consts.tile([P, P], F32)
+        make_identity(nc, ident[:])
+        identb = consts.tile([P, P], BF16)
+        make_identity(nc, identb[:])
+        bias_bc = consts.tile([P, WIDTH], BF16)
+        x_codes = consts.tile([P, MT * PASSES * P], U32, align_bytes=64)
+        x_scales = consts.tile([P, MT * PASSES * P], U8, align_bytes=64)
+        ab = consts.tile([P, MT, 2, HALF, 2], F32)
+        abrep = {}
+        for hc in sorted(set(CHUNKS)):
+            abrep[hc] = consts.tile([P, MT, hc, 4 * HALF], F32, name="abrep%d" % hc)
+
         def regroup(i):
             c, g = pieces[i]
             h0, hc = chunks[c]
-            src = raws[i][:].rearrange("p t (h y c i) -> p y h c t i", y=3, c=HS // 4, i=4)
-            made = []
-            for y in range(3):
-                grp = grpp.tile([P, 4 * HS * hc], BF16, name="grp", align_bytes=64)
-                dst = grp[:].rearrange("p (h c i t) -> p h c t i", c=HS // 4, i=4, t=4)
-                if y >= 3 - V_TYPES[i]:
-                    nc.vector.tensor_copy(out=dst, in_=src[:, y])
-                else:
-                    nc.scalar.copy(out=dst, in_=src[:, y])
-                made.append(grp)
-            groups[i] = made
+            by_head = raws[i][:].rearrange("p t (h r) -> p t h r", r=3 * HS)
+            gqk = grpp.tile([P, 8 * HS * hc], BF16, name="gqk", align_bytes=64)
+            nc.scalar.copy(
+                out=gqk[:].rearrange("p (h c i t) -> p h c t i", c=HS // 2, i=4, t=4),
+                in_=by_head[:, :, :, 0 : 2 * HS].rearrange("p t h (c i) -> p h c t i", i=4),
+            )
+            gv = grpp.tile([P, 4 * HS * hc], BF16, name="gv", align_bytes=64)
+            nc.vector.tensor_copy(
+                out=gv[:].rearrange("p (h c i t) -> p h c t i", c=HS // 4, i=4, t=4),
+                in_=by_head[:, :, :, 2 * HS : 3 * HS].rearrange("p t h (c i) -> p h c t i", i=4),
+            )
+            groups[i] = (gqk, gv)
 
         def quantise(i):
             c, g = pieces[i]
             h0, hc = chunks[c]
             if g == 0:
-                wc = codep.tile([P, PASSES, 3, HS * hc], U32, name="wc", align_bytes=64)
-                ws = codep.tile([P, PASSES, 3, HS * hc], U8, name="ws", align_bytes=64)
+                wc = codep.tile([P, PASSES, 3 * HS * hc], U32, name="wc", align_bytes=64)
+                ws = codep.tile([P, PASSES, 3 * HS * hc], U8, name="ws", align_bytes=64)
                 codes[c] = (wc, ws)
             wc, ws = codes[c]
-            for y in range(3):
-                nc.vector.quantize_mx(out=wc[:, g, y, :].bitcast(FP8X4), scales=ws[:, g, y, :], in_=groups[i][y][:])
+            gqk, gv = groups[i]
+            cut = 2 * HS * hc
+            nc.vector.quantize_mx(out=wc[:, g, cut:].bitcast(FP8X4), scales=ws[:, g, cut:], in_=gv[:])
+            nc.vector.quantize_mx(out=wc[:, g, 0:cut].bitcast(FP8X4), scales=ws[:, g, 0:cut], in_=gqk[:])
+
+        def bank_list(hc):
+            qk = [(m, 512 * b, 512) for m in range(MT) for b in range(hc // 2)]
+            return qk + [(m, 2 * HS * hc, HS * hc) for m in range(MT)]
 
         def matmuls(i):
             c, g = pieces[i]
             h0, hc = chunks[c]
             wc, ws = codes[c]
-            for m, y in ORDER:
+            for k, (m, lo_n, width) in enumerate(bank_list(hc)):
                 if g == 0:
-                    banks[(c, m, y)] = psum.tile([P, HS * hc], F32, name="acc%d%d" % (m, y))
+                    banks[(c, k)] = psum.tile([P, width], F32, name="acc%d" % k)
                 lo = (m * PASSES + g) * P
                 nc.tensor.matmul_mx(
-                    out=banks[(c, m, y)][:],
+                    out=banks[(c, k)][:],
                     lhsT=x_codes[:, lo : lo + P].bitcast(FP8X4),
                     lhsT_scale=x_scales[:, lo : lo + P],
-                    rhs=wc[:, g, y, :].bitcast(FP8X4),
-                    rhs_scale=ws[:, g, y, :],
+                    rhs=wc[:, g, lo_n : lo_n + width].bitcast(FP8X4),
+                    rhs_scale=ws[:, g, lo_n : lo_n + width],
                     start=(g == 0),
                     stop=(g == PASSES - 1),
                 )
@@ -142,23 +150,34 @@ def tile_gptneoxattention_pa_kernel(tc, x, w_qkv, b_qkv, cos, sin, out_0, out_1,
         def finish(c):
             h0, hc = chunks[c]
             st = stp.tile([P, 3, MT, HS * hc], F32, name="st%d" % c)
-            bias_v = bias_bc[:, 3 * HS * h0 : 3 * HS * (h0 + hc)].rearrange("p (h y f) -> p y h f", y=3, f=HS)
+            bias_v = bias_bc[:, 3 * HS * h0 : 3 * HS * (h0 + hc)].rearrange("p (h y f) -> p h y f", y=3, f=HS)
+            todo = bank_list(hc)
 
-            def leave(m, y):
-                nc.vector.tensor_tensor(
-                    out=st[:, y, m, :].rearrange("p (h f) -> p h f", f=HS),
-                    in0=banks[(c, m, y)][:].rearrange("p (h f) -> p h f", f=HS),
-                    in1=bias_v[:, y],
-                    op=ALU.add,
-                )
+            def leave(k):
+                m, lo_n, width = todo[k]
+                if lo_n < 2 * HS * hc:
+                    hh = lo_n // (2 * HS)
+                    nc.vector.tensor_tensor(
+                        out=st[:, 0:2, m, HS * hh : HS * (hh + 2)].rearrange("p y (h f) -> p h y f", f=HS),
+                        in0=banks[(c, k)][:].rearrange("p (h y f) -> p h y f", y=2, f=HS),
+                        in1=bias_v[:, hh : hh + 2, 0:2, :],
+                        op=ALU.add,
+                    )
+                else:
+                    nc.vector.tensor_tensor(
+                        out=st[:, 2, m, :].rearrange("p (h f) -> p h f", f=HS),
+                        in0=banks[(c, k)][:].rearrange("p (h f) -> p h f", f=HS),
+                        in1=bias_v[:, :, 2, :],
+                        op=ALU.add,
+                    )
 
             def store(y):
                 nc.sync.dma_start(
                     out=outs[y][0, :, h0 : h0 + hc, :].rearrange("(m p) h f -> p m (h f)", p=P), in_=st[:, y]
                 )
 
-            for m, y in ORDER[0:4]:
-                leave(m, y)
+            for k in range(len(todo) - 2):
+                leave(k)
             shape = [P, 2, MT * hc, 2 * HALF, 2]
             prod = prodp.tile(shape, F32, name="prod")
             nc.vector.tensor_tensor(
@@ -167,7 +186,7 @@ def tile_gptneoxattention_pa_kernel(tc, x, w_qkv, b_qkv, cos, sin, out_0, out_1,
                 in1=abrep[hc][:].rearrange("p m h (a e) -> p (m h) a e", e=2).unsqueeze(1).to_broadcast(shape),
                 op=ALU.mult,
             )
-            leave(0, 2)
+            leave(len(todo) - 2)
             flat = prod[:].rearrange("p y g a e -> p (y g) (a e)")
             nc.vector.tensor_tensor(
                 out=st[:, 0:2].rearrange("p y m (h f) -> p (y m h) f", f=HS)[:, :, 0 : 2 * HALF],
@@ -177,62 +196,47 @@ def tile_gptneoxattention_pa_kernel(tc, x, w_qkv, b_qkv, cos, sin, out_0, out_1,
             )
             store(0)
             store(1)
-            leave(1, 2)
+            leave(len(todo) - 1)
             store(2)
 
-        x_sb = None
-        for i in range(DEPTH - 1):
-            load_next()
-            if i == X_AFTER:
-                x_sb = rawp.tile([P, MT, D], BF16, name="raw")
-                for m in range(MT):
-                    nc.sync.dma_start(out=x_sb[:, m, :], in_=x[0, P * m : P * (m + 1), :])
-
-        pbs = []
-        for k in range(WIDTH // 1024):
-            m, y = ORDER[k]
-            pb = psum.tile([P, 1024], BF16, name="pb%d" % k, tag="acc%d%d" % (m, y))
-            for j in range(2):
-                r = 2 * k + j
-                nc.tensor.matmul(
-                    out=pb[:, 512 * j : 512 * (j + 1)],
-                    lhsT=identb[:, r : r + 1].to_broadcast([P, P]),
-                    rhs=b12[:],
-                    start=True,
-                    stop=True,
-                )
-            pbs.append(pb)
-
-        def bias_out():
-            for k in range(WIDTH // 1024):
-                if B_ENG == "S":
-                    nc.scalar.copy(out=bias_bc[:, 1024 * k : 1024 * (k + 1)], in_=pbs[k][:])
-                else:
-                    nc.vector.tensor_copy(out=bias_bc[:, 1024 * k : 1024 * (k + 1)], in_=pbs[k][:])
-
-        gxs = []
+        gx = {}
 
         def x_transposes():
+            gx[0] = grpp.tile([P, MT, 4 * PASSES * P], BF16, name="gqk", align_bytes=64)
             for m in range(MT):
                 words = x_sb[:, m, :].bitcast(F32).rearrange("p (g c u) -> p g u c", g=PASSES, u=2)
-                gx = grpp.tile([P, 4 * PASSES * P], BF16, name="grp", align_bytes=64)
-                gxw = gx[:].bitcast(F32).rearrange("p (g r u) -> p g r u", g=PASSES, u=2)
+                gxw = gx[0][:, m, :].bitcast(F32).rearrange("p (g r u) -> p g r u", g=PASSES, u=2)
                 for gp in range(PASSES // 2):
                     xt = psum.tile([P, 2, 2, P], F32, name="pt", bufs=2)
                     for gl in range(2):
                         for u in range(2):
                             nc.tensor.transpose(xt[:, gl, u, :], words[:, 2 * gp + gl, u, :], ident[:])
-                    nc.vector.tensor_copy(out=gxw[:, 2 * gp : 2 * gp + 2], in_=xt[:].rearrange("p g u r -> p g r u"))
-                gxs.append(gx)
+                    nc.scalar.copy(out=gxw[:, 2 * gp : 2 * gp + 2], in_=xt[:].rearrange("p g u r -> p g r u"))
+
+        pbs = []
+
+        def bias_matmuls():
+            for k in range(WIDTH // 1024):
+                pb = psum.tile([P, 1024], BF16, name="pb%d" % k, tag="acc%d" % k)
+                for j in range(2):
+                    r = 2 * k + j
+                    nc.tensor.matmul(
+                        out=pb[:, 512 * j : 512 * (j + 1)],
+                        lhsT=identb[:, r : r + 1].to_broadcast([P, P]),
+                        rhs=b12[:],
+                        start=True,
+                        stop=True,
+                    )
+                pbs.append(pb)
+
+        def bias_out():
+            for k in range(WIDTH // 1024):
+                nc.vector.tensor_copy(out=bias_bc[:, 1024 * k : 1024 * (k + 1)], in_=pbs[k][:])
 
         def x_quantise():
-            for m in range(MT):
-                lo = m * PASSES * P
-                nc.vector.quantize_mx(
-                    out=x_codes[:, lo : lo + PASSES * P].bitcast(FP8X4),
-                    scales=x_scales[:, lo : lo + PASSES * P],
-                    in_=gxs[m][:],
-                )
+            nc.vector.quantize_mx(
+                out=x_codes[:].bitcast(FP8X4), scales=x_scales[:], in_=gx[0][:].rearrange("p m k -> p (m k)")
+            )
 
         def tables():
             nc.vector.tensor_copy(out=ab[:, :, 0, :, 0], in_=cs[:, 0])
@@ -246,22 +250,23 @@ def tile_gptneoxattention_pa_kernel(tc, x, w_qkv, b_qkv, cos, sin, out_0, out_1,
                 )
 
         pend = []
-        for i in range(n + LAG):
+        for i in range(n + 1):
             if i < n:
                 regroup(i)
                 load_next()
-            if i == X_STEP - 1:
+            if i == X_STEP:
                 x_transposes()
                 load_next()
+                bias_matmuls()
+            if i == X_STEP + 1:
+                x_quantise()
             if i == B_STEP:
                 bias_out()
                 tables()
-            if i == X_STEP:
-                x_quantise()
-            if i - LAG >= 0:
-                quantise(i - LAG)
-                pend.append(i - LAG)
-            if i >= X_STEP and i >= B_STEP:
+            if i >= 1:
+                quantise(i - 1)
+                pend.append(i - 1)
+            if i >= B_STEP:
                 for j in pend:
                     matmuls(j)
                     if pieces[j][1] == PASSES - 1:

@@ -101,9 +101,24 @@ def tile_gptneoxattention_pa_kernel(tc, x, w_qkv, b_qkv, cos, sin, out_0, out_1,
             h0, hc = chunks[c]
             by_head = raws[i][:].rearrange("p t (h r) -> p t h r", r=3 * HS)
             gqk = grpp.tile([P, 8 * HS * hc], BF16, name="gqk", align_bytes=64)
+            via_pe = 1 if hc == 4 else 0
+            direct = hc - via_pe
+            if via_pe:
+                woven = psum.tile([P, 2, HS, 4], BF16, name="pt", bufs=2)
+                for y in range(2):
+                    nc.tensor.matmul(
+                        out=woven[:, y],
+                        lhsT=identb[:],
+                        rhs=by_head[:, :, direct, HS * y : HS * (y + 1)].rearrange("p t n -> p n t"),
+                        start=True,
+                        stop=True,
+                    )
+                nc.scalar.copy(
+                    out=gqk[:, 8 * HS * direct : 8 * HS * hc], in_=woven[:].rearrange("p y n t -> p (y n t)")
+                )
             nc.scalar.copy(
-                out=gqk[:].rearrange("p (h c i t) -> p h c t i", c=HS // 2, i=4, t=4),
-                in_=by_head[:, :, :, 0 : 2 * HS].rearrange("p t h (c i) -> p h c t i", i=4),
+                out=gqk[:].rearrange("p (h c i t) -> p h c t i", c=HS // 2, i=4, t=4)[:, 0:direct],
+                in_=by_head[:, :, 0:direct, 0 : 2 * HS].rearrange("p t h (c i) -> p h c t i", i=4),
             )
             gv = grpp.tile([P, 4 * HS * hc], BF16, name="gv", align_bytes=64)
             nc.vector.tensor_copy(

@@ -21,7 +21,6 @@ PASSES = D // (4 * P)
 HALF = 16
 FLOPS = 2 * TOK * D * WIDTH
 
-PINNED = False
 CHUNKS = [2,4,4,4,2]
 DEPTH = 5
 X_STEP = 1
@@ -39,8 +38,7 @@ def tile_gptneoxattention_pa_kernel(tc, x, w_qkv, b_qkv, cos, sin, out_0, out_1,
         stp = ctx.enter_context(tc.tile_pool(name="stp", bufs=1))
         prodp = ctx.enter_context(tc.tile_pool(name="prodp", bufs=1))
         psum = ctx.enter_context(tc.psum_pool(name="psum", bufs=1))
-        if PINNED:
-            ctx.enter_context(tc.manual_schedule())
+        ctx.enter_context(tc.manual_schedule(engines={mybir.EngineType.SP}))
 
         chunks = []
         first = 0
@@ -162,6 +160,13 @@ def tile_gptneoxattention_pa_kernel(tc, x, w_qkv, b_qkv, cos, sin, out_0, out_1,
                     stop=(g == PASSES - 1),
                 )
 
+        waiting = []
+
+        def flush_stores():
+            for dst, src in waiting:
+                nc.sync.dma_start(out=dst, in_=src)
+            waiting.clear()
+
         def finish(c):
             h0, hc = chunks[c]
             st = stp.tile([P, 3, MT, HS * hc], F32, name="st%d" % c)
@@ -187,9 +192,9 @@ def tile_gptneoxattention_pa_kernel(tc, x, w_qkv, b_qkv, cos, sin, out_0, out_1,
                     )
 
             def store(y):
-                nc.sync.dma_start(
-                    out=outs[y][0, :, h0 : h0 + hc, :].rearrange("(m p) h f -> p m (h f)", p=P), in_=st[:, y]
-                )
+                waiting.append((outs[y][0, :, h0 : h0 + hc, :].rearrange("(m p) h f -> p m (h f)", p=P), st[:, y]))
+                if state["next"] >= n:
+                    flush_stores()
 
             for k in range(len(todo) - 2):
                 leave(k)
@@ -269,6 +274,8 @@ def tile_gptneoxattention_pa_kernel(tc, x, w_qkv, b_qkv, cos, sin, out_0, out_1,
             if i < n:
                 regroup(i)
                 load_next()
+                if state["next"] >= n:
+                    flush_stores()
             if i == X_STEP:
                 x_transposes()
                 load_next()

@@ -25,6 +25,7 @@ CHUNKS = [2,4,4,4,2]
 DEPTH = 5
 X_STEP = 1
 B_STEP = 3
+BIAS_BANKS_ON_VECTOR = 2
 
 
 def tile_gptneoxattention_pa_kernel(tc, x, w_qkv, b_qkv, cos, sin, out_0, out_1, out_2):
@@ -101,6 +102,10 @@ def tile_gptneoxattention_pa_kernel(tc, x, w_qkv, b_qkv, cos, sin, out_0, out_1,
             gqk = grpp.tile([P, 8 * HS * hc], BF16, name="gqk", align_bytes=64)
             via_pe = 1 if hc == 4 else 0
             direct = hc - via_pe
+            nc.scalar.copy(
+                out=gqk[:].rearrange("p (h c i t) -> p h c t i", c=HS // 2, i=4, t=4)[:, 0:direct],
+                in_=by_head[:, :, 0:direct, 0 : 2 * HS].rearrange("p t h (c i) -> p h c t i", i=4),
+            )
             if via_pe:
                 woven = psum.tile([P, 2, HS, 4], BF16, name="pt", bufs=2)
                 for y in range(2):
@@ -112,12 +117,9 @@ def tile_gptneoxattention_pa_kernel(tc, x, w_qkv, b_qkv, cos, sin, out_0, out_1,
                         stop=True,
                     )
                 nc.scalar.copy(
-                    out=gqk[:, 8 * HS * direct : 8 * HS * hc], in_=woven[:].rearrange("p y n t -> p (y n t)")
+                    out=gqk[:, 8 * HS * direct : 8 * HS * hc].bitcast(F32),
+                    in_=woven[:].rearrange("p y n t -> p (y n t)").bitcast(F32),
                 )
-            nc.scalar.copy(
-                out=gqk[:].rearrange("p (h c i t) -> p h c t i", c=HS // 2, i=4, t=4)[:, 0:direct],
-                in_=by_head[:, :, 0:direct, 0 : 2 * HS].rearrange("p t h (c i) -> p h c t i", i=4),
-            )
             gv = grpp.tile([P, 4 * HS * hc], BF16, name="gv", align_bytes=64)
             nc.vector.tensor_copy(
                 out=gv[:].rearrange("p (h c i t) -> p h c t i", c=HS // 4, i=4, t=4),
@@ -251,7 +253,12 @@ def tile_gptneoxattention_pa_kernel(tc, x, w_qkv, b_qkv, cos, sin, out_0, out_1,
 
         def bias_out():
             for k in range(WIDTH // 1024):
-                nc.vector.tensor_copy(out=bias_bc[:, 1024 * k : 1024 * (k + 1)], in_=pbs[k][:])
+                if k < BIAS_BANKS_ON_VECTOR:
+                    nc.vector.tensor_copy(out=bias_bc[:, 1024 * k : 1024 * (k + 1)], in_=pbs[k][:])
+                else:
+                    nc.scalar.copy(
+                        out=bias_bc[:, 1024 * k : 1024 * (k + 1)].bitcast(F32), in_=pbs[k][:].bitcast(F32)
+                    )
 
         def x_quantise():
             nc.vector.quantize_mx(

from contextlib import ExitStack

import concourse.mybir as mybir
from concourse.masks import make_identity

FP8X4 = mybir.dt.float8_e4m3fn_x4
BF16 = mybir.dt.bfloat16
F32 = mybir.dt.float32
U32 = mybir.dt.uint32
U8 = mybir.dt.uint8
ALU = mybir.AluOpType

P = 128
TOK = 256
D = 2048
HEADS = 16
HS = 128
WIDTH = 3 * HEADS * HS
MT = TOK // P
PASSES = D // (4 * P)
HALF = 16
FLOPS = 2 * TOK * D * WIDTH

CHUNKS = [2,4,4,4,2]
DEPTH = 5
X_STEP = 1
B_STEP = 3
BIAS_BANKS_ON_VECTOR = 2


def tile_gptneoxattention_pa_kernel(tc, x, w_qkv, b_qkv, cos, sin, out_0, out_1, out_2):
    nc = tc.nc
    outs = [out_0, out_1, out_2]
    with ExitStack() as ctx:
        consts = ctx.enter_context(tc.tile_pool(name="consts", bufs=1))
        rawp = ctx.enter_context(tc.tile_pool(name="rawp", bufs=DEPTH))
        grpp = ctx.enter_context(tc.tile_pool(name="grpp", bufs=3))
        codep = ctx.enter_context(tc.tile_pool(name="codep", bufs=2))
        stp = ctx.enter_context(tc.tile_pool(name="stp", bufs=1))
        prodp = ctx.enter_context(tc.tile_pool(name="prodp", bufs=1))
        psum = ctx.enter_context(tc.psum_pool(name="psum", bufs=1))
        ctx.enter_context(tc.manual_schedule(engines={mybir.EngineType.SP}))

        chunks = []
        first = 0
        for hc in CHUNKS:
            chunks.append((first, hc))
            first += hc
        pieces = [(c, g) for c in range(len(chunks)) for g in range(PASSES)]
        n = len(pieces)

        raws = {}
        groups = {}
        codes = {}
        banks = {}
        state = {"next": 0}

        def load_next():
            i = state["next"]
            if i >= n:
                return
            state["next"] = i + 1
            c, g = pieces[i]
            h0, hc = chunks[c]
            raw = rawp.tile([P, 4, 3 * HS * hc], BF16, name="raw")
            nc.sync.dma_start(
                out=raw[:],
                in_=w_qkv[4 * P * g : 4 * P * (g + 1), 3 * HS * h0 : 3 * HS * (h0 + hc)].rearrange(
                    "(p j) n -> p j n", j=4
                ),
            )
            raws[i] = raw

        b12 = consts.tile([P, 512], BF16)
        nc.vector.memset(b12[:].bitcast(F32), 0.0)
        load_next()
        nc.sync.dma_start(out=b12[0 : WIDTH // 512, :], in_=b_qkv.rearrange("(k n) -> k n", n=512))
        x_sb = rawp.tile([P, MT, D], BF16, name="raw")
        for m in range(MT):
            nc.sync.dma_start(out=x_sb[:, m, :], in_=x[0, P * m : P * (m + 1), :])
        for i in range(DEPTH - 2):
            load_next()
        cs = consts.tile([P, 2, MT, HALF], BF16)
        nc.scalar.dma_start(out=cs[:, 0], in_=cos.rearrange("(m p) j -> p m j", p=P))
        nc.scalar.dma_start(out=cs[:, 1], in_=sin.rearrange("(m p) j -> p m j", p=P))
        ident = consts.tile([P, P], F32)
        make_identity(nc, ident[:])
        identb = consts.tile([P, P], BF16)
        make_identity(nc, identb[:])
        bias_bc = consts.tile([P, WIDTH], BF16)
        x_codes = consts.tile([P, MT * PASSES * P], U32, align_bytes=64)
        x_scales = consts.tile([P, MT * PASSES * P], U8, align_bytes=64)
        ab = consts.tile([P, MT, 2, HALF, 2], F32)
        abrep = {}
        for hc in sorted(set(CHUNKS)):
            abrep[hc] = consts.tile([P, MT, hc, 4 * HALF], F32, name="abrep%d" % hc)

        def regroup(i):
            c, g = pieces[i]
            h0, hc = chunks[c]
            by_head = raws[i][:].rearrange("p t (h r) -> p t h r", r=3 * HS)
            gqk = grpp.tile([P, 8 * HS * hc], BF16, name="gqk", align_bytes=64)
            via_pe = 1 if hc == 4 else 0
            direct = hc - via_pe
            nc.scalar.copy(
                out=gqk[:].rearrange("p (h c i t) -> p h c t i", c=HS // 2, i=4, t=4)[:, 0:direct],
                in_=by_head[:, :, 0:direct, 0 : 2 * HS].rearrange("p t h (c i) -> p h c t i", i=4),
            )
            if via_pe:
                woven = psum.tile([P, 2, HS, 4], BF16, name="pt", bufs=2)
                for y in range(2):
                    nc.tensor.matmul(
                        out=woven[:, y],
                        lhsT=identb[:],
                        rhs=by_head[:, :, direct, HS * y : HS * (y + 1)].rearrange("p t n -> p n t"),
                        start=True,
                        stop=True,
                    )
                nc.scalar.copy(
                    out=gqk[:, 8 * HS * direct : 8 * HS * hc].bitcast(F32),
                    in_=woven[:].rearrange("p y n t -> p (y n t)").bitcast(F32),
                )
            gv = grpp.tile([P, 4 * HS * hc], BF16, name="gv", align_bytes=64)
            nc.vector.tensor_copy(
                out=gv[:].rearrange("p (h c i t) -> p h c t i", c=HS // 4, i=4, t=4),
                in_=by_head[:, :, :, 2 * HS : 3 * HS].rearrange("p t h (c i) -> p h c t i", i=4),
            )
            groups[i] = (gqk, gv)

        def quantise(i):
            c, g = pieces[i]
            h0, hc = chunks[c]
            if g == 0:
                wc = codep.tile([P, PASSES, 3 * HS * hc], U32, name="wc", align_bytes=64)
                ws = codep.tile([P, PASSES, 3 * HS * hc], U8, name="ws", align_bytes=64)
                codes[c] = (wc, ws)
            wc, ws = codes[c]
            gqk, gv = groups[i]
            cut = 2 * HS * hc
            nc.vector.quantize_mx(out=wc[:, g, cut:].bitcast(FP8X4), scales=ws[:, g, cut:], in_=gv[:])
            nc.vector.quantize_mx(out=wc[:, g, 0:cut].bitcast(FP8X4), scales=ws[:, g, 0:cut], in_=gqk[:])

        def bank_list(hc):
            qk = [(m, 512 * b, 512) for m in range(MT) for b in range(hc // 2)]
            return qk + [(m, 2 * HS * hc, HS * hc) for m in range(MT)]

        def matmuls(i):
            c, g = pieces[i]
            h0, hc = chunks[c]
            wc, ws = codes[c]
            for k, (m, lo_n, width) in enumerate(bank_list(hc)):
                if g == 0:
                    banks[(c, k)] = psum.tile([P, width], F32, name="acc%d" % k)
                lo = (m * PASSES + g) * P
                nc.tensor.matmul_mx(
                    out=banks[(c, k)][:],
                    lhsT=x_codes[:, lo : lo + P].bitcast(FP8X4),
                    lhsT_scale=x_scales[:, lo : lo + P],
                    rhs=wc[:, g, lo_n : lo_n + width].bitcast(FP8X4),
                    rhs_scale=ws[:, g, lo_n : lo_n + width],
                    start=(g == 0),
                    stop=(g == PASSES - 1),
                )

        waiting = []

        def flush_stores():
            for dst, src in waiting:
                nc.sync.dma_start(out=dst, in_=src)
            waiting.clear()

        def finish(c):
            h0, hc = chunks[c]
            st = stp.tile([P, 3, MT, HS * hc], F32, name="st%d" % c)
            bias_v = bias_bc[:, 3 * HS * h0 : 3 * HS * (h0 + hc)].rearrange("p (h y f) -> p h y f", y=3, f=HS)
            todo = bank_list(hc)

            def leave(k):
                m, lo_n, width = todo[k]
                if lo_n < 2 * HS * hc:
                    hh = lo_n // (2 * HS)
                    nc.vector.tensor_tensor(
                        out=st[:, 0:2, m, HS * hh : HS * (hh + 2)].rearrange("p y (h f) -> p h y f", f=HS),
                        in0=banks[(c, k)][:].rearrange("p (h y f) -> p h y f", y=2, f=HS),
                        in1=bias_v[:, hh : hh + 2, 0:2, :],
                        op=ALU.add,
                    )
                else:
                    nc.vector.tensor_tensor(
                        out=st[:, 2, m, :].rearrange("p (h f) -> p h f", f=HS),
                        in0=banks[(c, k)][:].rearrange("p (h f) -> p h f", f=HS),
                        in1=bias_v[:, :, 2, :],
                        op=ALU.add,
                    )

            def store(y):
                waiting.append((outs[y][0, :, h0 : h0 + hc, :].rearrange("(m p) h f -> p m (h f)", p=P), st[:, y]))
                if state["next"] >= n:
                    flush_stores()

            for k in range(len(todo) - 2):
                leave(k)
            shape = [P, 2, MT * hc, 2 * HALF, 2]
            prod = prodp.tile(shape, F32, name="prod")
            nc.vector.tensor_tensor(
                out=prod[:],
                in0=st[:, 0:2].rearrange("p y m (h f) -> p y (m h) f", f=HS)[:, :, :, 0 : 2 * HALF].unsqueeze(4).to_broadcast(shape),
                in1=abrep[hc][:].rearrange("p m h (a e) -> p (m h) a e", e=2).unsqueeze(1).to_broadcast(shape),
                op=ALU.mult,
            )
            leave(len(todo) - 2)
            flat = prod[:].rearrange("p y g a e -> p (y g) (a e)")
            nc.vector.tensor_tensor(
                out=st[:, 0:2].rearrange("p y m (h f) -> p (y m h) f", f=HS)[:, :, 0 : 2 * HALF],
                in0=flat[:, :, 0 : 2 * HALF],
                in1=flat[:, :, 2 * HALF : 4 * HALF],
                op=ALU.add,
            )
            store(0)
            store(1)
            leave(len(todo) - 1)
            store(2)

        gx = {}

        def x_transposes():
            gx[0] = grpp.tile([P, MT, 4 * PASSES * P], BF16, name="gqk", align_bytes=64)
            for m in range(MT):
                words = x_sb[:, m, :].bitcast(F32).rearrange("p (g c u) -> p g u c", g=PASSES, u=2)
                gxw = gx[0][:, m, :].bitcast(F32).rearrange("p (g r u) -> p g r u", g=PASSES, u=2)
                for gp in range(PASSES // 2):
                    xt = psum.tile([P, 2, 2, P], F32, name="pt", bufs=2)
                    for gl in range(2):
                        for u in range(2):
                            nc.tensor.transpose(xt[:, gl, u, :], words[:, 2 * gp + gl, u, :], ident[:])
                    nc.scalar.copy(out=gxw[:, 2 * gp : 2 * gp + 2], in_=xt[:].rearrange("p g u r -> p g r u"))

        pbs = []

        def bias_matmuls():
            for k in range(WIDTH // 1024):
                pb = psum.tile([P, 1024], BF16, name="pb%d" % k, tag="acc%d" % k)
                for j in range(2):
                    r = 2 * k + j
                    nc.tensor.matmul(
                        out=pb[:, 512 * j : 512 * (j + 1)],
                        lhsT=identb[:, r : r + 1].to_broadcast([P, P]),
                        rhs=b12[:],
                        start=True,
                        stop=True,
                    )
                pbs.append(pb)

        def bias_out():
            for k in range(WIDTH // 1024):
                if k < BIAS_BANKS_ON_VECTOR:
                    nc.vector.tensor_copy(out=bias_bc[:, 1024 * k : 1024 * (k + 1)], in_=pbs[k][:])
                else:
                    nc.scalar.copy(
                        out=bias_bc[:, 1024 * k : 1024 * (k + 1)].bitcast(F32), in_=pbs[k][:].bitcast(F32)
                    )

        def x_quantise():
            nc.vector.quantize_mx(
                out=x_codes[:].bitcast(FP8X4), scales=x_scales[:], in_=gx[0][:].rearrange("p m k -> p (m k)")
            )

        def tables():
            nc.vector.tensor_copy(out=ab[:, :, 0, :, 0], in_=cs[:, 0])
            nc.vector.tensor_copy(out=ab[:, :, 0, :, 1], in_=cs[:, 1])
            nc.vector.tensor_scalar_mul(out=ab[:, :, 1, :, 0], in0=cs[:, 1], scalar1=-1.0)
            nc.vector.tensor_copy(out=ab[:, :, 1, :, 1], in_=cs[:, 0])
            for hc in sorted(set(CHUNKS)):
                nc.vector.tensor_copy(
                    out=abrep[hc][:],
                    in_=ab[:].rearrange("p m a j e -> p m (a j e)").unsqueeze(2).to_broadcast([P, MT, hc, 4 * HALF]),
                )

        pend = []
        for i in range(n + 1):
            if i < n:
                regroup(i)
                load_next()
                if state["next"] >= n:
                    flush_stores()
            if i == X_STEP:
                x_transposes()
                load_next()
                bias_matmuls()
            if i == X_STEP + 1:
                x_quantise()
            if i == B_STEP:
                bias_out()
                tables()
            if i >= 1:
                quantise(i - 1)
                pend.append(i - 1)
            if i >= B_STEP:
                for j in pend:
                    matmuls(j)
                    if pieces[j][1] == PASSES - 1:
                        finish(pieces[j][0])
                pend = []
